import numpy as np
import ml_dtypes


def mxq(x, axis, fmt="e4m3"):
    dtype, down = {"e4m3": (ml_dtypes.float8_e4m3fn, 7), "e5m2": (ml_dtypes.float8_e5m2, 14)}[fmt]
    v = np.moveaxis(np.asarray(x, np.float32).astype(ml_dtypes.bfloat16).astype(np.float64), axis, -1)
    blocks = v.reshape(v.shape[:-1] + (-1, 32))
    amax = np.abs(blocks).max(-1, keepdims=True)
    byte = np.maximum(np.where(amax > 0, np.frexp(amax)[1] - 1 + 127, 0) - down, 1)
    scale = np.exp2(byte - 127.0)
    codes = (blocks / scale).astype(np.float32).astype(dtype).astype(np.float64)
    return np.moveaxis((codes * scale).reshape(v.shape), -1, axis)


WIDE = False


def mx_kscale(k):
    if not WIDE:
        return np.ones(k)
    levels = np.array([10, -10, 5, -5, 0])
    if k % 512:
        return np.exp2(np.random.permutation(np.resize(levels, k // 32))).repeat(32)
    a = np.empty((k // 512, 16))
    for p in range(k // 512):
        a[p, :8] = np.random.permutation(np.resize(levels, 8))
        for g in range(8):
            far = levels[np.abs(levels - a[p, g]) >= 10]
            a[p, g + 8] = far[np.random.randint(len(far))]
    return np.exp2(a.ravel()).repeat(32)


BF16 = ml_dtypes.bfloat16


def bf(x):
    return np.asarray(x, np.float32).astype(BF16)


def f64(x):
    return np.asarray(x).astype(np.float64)


B, V, K, C = 2, 4096, 512, 512


def setup_inputs():
    s = mx_kscale(K)
    u = np.exp2(np.round(np.log2(s / s.max()) / 2))
    return {"evals": bf(np.random.uniform(0.0, 4.0, (B, K)) + np.log(u * u)),
            "evecs": bf(np.random.standard_normal((B, V, K)) * 2.0 / np.sqrt(K) * u),
            "count": C}


def reference(evals, evecs, count):
    scales = 10.0 ** np.linspace(-2.0, 0.0, count)
    coefs = np.exp(-f64(evals)[:, None, :] * scales[None, :, None])
    ev = f64(evecs)
    sq = ev * ev
    return mxq(sq, 2, "e4m3") @ mxq(coefs, 2, "e4m3").transpose(0, 2, 1)

@@ -1,0 +1,192 @@
+from contextlib import ExitStack
+
+import concourse.mybir as mybir
+from concourse.masks import make_identity
+
+F32 = mybir.dt.float32
+BF16 = mybir.dt.bfloat16
+U32 = mybir.dt.uint32
+U8 = mybir.dt.uint8
+FP8X4 = mybir.dt.float8_e4m3fn_x4
+ACT = mybir.ActivationFunctionType
+ALU = mybir.AluOpType
+
+P = 128
+B, V, K, C = 2, 4096, 512, 512
+TILES = V // P
+GROUPS = [4] * 15 + [2, 2]
+NG = len(GROUPS)
+FIRST = [sum(GROUPS[:g]) for g in range(NG)]
+
+FLOPS = 2 * B * V * K * C
+
+LOADS = [(0, 0, 2), (0, 2, 2), (0, 4, 4), (0, 8, 8), (0, 16, 16), (1, 0, 32)]
+STAGE_BUFS = 10
+SCALAR_COPIES = [0, 0, 0, 0, 0, 0, 1, 0, 1, 0, 1, 0, 1, 1, 2, 1, 1]
+EXP1_AFTER = 3
+QUANT1_AT = 5
+
+
+def tile_hks_t_kernel(tc, evals, evecs, count, out):
+    nc = tc.nc
+    assert tuple(evecs.shape) == (B, V, K) and count == C
+
+    with ExitStack() as ctx:
+        consts = ctx.enter_context(tc.tile_pool(name="consts", bufs=1))
+        xpool = ctx.enter_context(tc.tile_pool(name="xpool", bufs=1))
+        gpool = ctx.enter_context(tc.tile_pool(name="gpool", bufs=3))
+        spool = ctx.enter_context(tc.tile_pool(name="spool", bufs=STAGE_BUFS))
+        psum = ctx.enter_context(tc.psum_pool(name="psum", bufs=4))
+        ctx.enter_context(tc.manual_schedule())
+
+        ev = consts.tile([P, 4 * B], BF16, name="ev")
+        with nc.allow_non_contiguous_dma(reason="evals: four neighbouring values to a partition"):
+            nc.sync.dma_start(
+                out=ev[:].rearrange("p (b t) -> p b t", b=B, t=4),
+                in_=evals.rearrange("b (p t) -> p b t", p=P, t=4),
+            )
+        words = {}
+        for b, t0, n in LOADS:
+            x = xpool.tile([P, n * K], BF16, name="x_%d_%d" % (b, t0))
+            src = evecs[b].rearrange("(p t) k -> p (t k)", t=TILES)
+            nc.sync.dma_start(out=x[:], in_=src[:, t0 * K : (t0 + n) * K])
+            xw = x[:].bitcast(F32)
+            for j in range(n):
+                words[b * TILES + t0 + j] = xw[:, j * (K // 2) : (j + 1) * (K // 2)]
+
+        ident = consts.tile([P, P], F32, name="ident")
+        make_identity(nc, ident[:])
+
+        powers = consts.tile([P, C], F32, name="powers")
+        nc.vector.memset(powers[:, 0:1], 1.0)
+        warm = consts.tile([P, 1], F32, name="warm")
+        nc.scalar.activation(out=warm[:], in_=powers[:, 0:1], func=ACT.Exp)
+        n = 1
+        while n < C:
+            nc.vector.tensor_scalar(
+                out=powers[:, n : 2 * n],
+                in0=powers[:, 0:n],
+                scalar1=10.0 ** (2.0 * n / (C - 1)),
+                scalar2=None,
+                op0=ALU.mult,
+            )
+            n *= 2
+
+        args = {}
+        coef_codes = {}
+        coef_scales = {}
+
+        def coef_args(b):
+            a = consts.tile([P, 4 * C], F32, name="arg%d" % b)
+            nc.vector.tensor_tensor(
+                out=a[:].rearrange("p (c t) -> p c t", t=4),
+                in0=powers[:].unsqueeze(2).to_broadcast([P, C, 4]),
+                in1=ev[:, 4 * b : 4 * b + 4].unsqueeze(1).to_broadcast([P, C, 4]),
+                op=ALU.mult,
+            )
+            args[b] = a
+
+        def coef_exp(b):
+            cf = consts.tile([P, 4 * C], BF16, name="cf%d" % b, align_bytes=64)
+            nc.scalar.activation(out=cf[:], in_=args[b][:], func=ACT.Exp, scale=-0.01)
+            args[b] = cf
+
+        def coef_quant(b):
+            cc = consts.tile([P, C], U32, name="cc%d" % b, align_bytes=64)
+            cs = consts.tile([P, C], U8, name="cs%d" % b, align_bytes=64)
+            nc.vector.quantize_mx(out=cc[:].bitcast(FP8X4), scales=cs[:], in_=args[b][:])
+            coef_codes[b] = cc
+            coef_scales[b] = cs
+
+        banks = {}
+        grouped = {}
+        codes = {}
+        scales = {}
+        accs = {}
+
+        def transposes(g):
+            banks[g] = []
+            for h in range(GROUPS[g] // 2):
+                xt = psum.tile([P, 512], F32, name="xt", tag="xt")
+                for vt in range(2):
+                    src = words[FIRST[g] + 2 * h + vt]
+                    for u in range(2):
+                        lo = u * 256 + vt * P
+                        nc.tensor.transpose(xt[:, lo : lo + P], src[:, u : K // 2 : 2], ident[:])
+                banks[g].append(xt)
+
+        def squares(g):
+            grp = gpool.tile([P, GROUPS[g] * K], BF16, name="grouped", tag="grouped", align_bytes=64)
+            for h in range(GROUPS[g] // 2):
+                nc.scalar.activation(
+                    out=grp[:, h * 1024 : (h + 1) * 1024].rearrange("p (c u e) -> p c u e", u=2, e=2),
+                    in_=banks[g][h][:].bitcast(BF16).rearrange("p (u c e) -> p c u e", u=2, e=2),
+                    func=ACT.Square,
+                )
+            grouped[g] = grp
+
+        def quantise(g):
+            cd = gpool.tile([P, GROUPS[g] * P], U32, name="codes", tag="codes", align_bytes=64)
+            sc = gpool.tile([P, GROUPS[g] * P], U8, name="scales", tag="scales", align_bytes=64)
+            nc.vector.quantize_mx(out=cd[:].bitcast(FP8X4), scales=sc[:], in_=grouped[g][:])
+            codes[g] = cd
+            scales[g] = sc
+
+        def multiply(g):
+            b = FIRST[g] // TILES
+            accs[g] = []
+            for j in range(GROUPS[g]):
+                acc = psum.tile([P, C], F32, name="acc", tag="acc")
+                nc.tensor.matmul_mx(
+                    out=acc[:],
+                    lhsT=codes[g][:, j * P : (j + 1) * P].bitcast(FP8X4),
+                    lhsT_scale=scales[g][:, j * P : (j + 1) * P],
+                    rhs=coef_codes[b][:].bitcast(FP8X4),
+                    rhs_scale=coef_scales[b][:],
+                    start=True,
+                    stop=True,
+                )
+                accs[g].append(acc)
+
+        stages = {}
+
+        def vector_copies(g):
+            stage = spool.tile([P, GROUPS[g] * C], F32, name="stage", tag="stage")
+            for j in range(GROUPS[g] - SCALAR_COPIES[g]):
+                nc.vector.tensor_copy(out=stage[:, j * C : (j + 1) * C], in_=accs[g][j][:])
+            stages[g] = stage
+
+        def scalar_copies_and_store(g):
+            b = FIRST[g] // TILES
+            t0 = FIRST[g] % TILES
+            stage = stages[g]
+            for j in range(GROUPS[g] - SCALAR_COPIES[g], GROUPS[g]):
+                nc.scalar.copy(out=stage[:, j * C : (j + 1) * C], in_=accs[g][j][:])
+            dram = out[b].rearrange("(p t) c -> p (t c)", t=TILES)
+            nc.sync.dma_start(out=dram[:, t0 * C : (t0 + GROUPS[g]) * C], in_=stage[:])
+
+        coef_args(0)
+        coef_args(1)
+        transposes(0)
+        transposes(1)
+        squares(0)
+        coef_exp(0)
+        for g in range(NG):
+            quantise(g)
+            if g == 0:
+                coef_quant(0)
+            if g + 2 < NG:
+                transposes(g + 2)
+            if g > 0:
+                vector_copies(g - 1)
+            if g == QUANT1_AT:
+                coef_quant(1)
+            if g + 1 < NG:
+                squares(g + 1)
+            if g > 0:
+                scalar_copies_and_store(g - 1)
+            if g == EXP1_AFTER:
+                coef_exp(1)
+            multiply(g)
+        vector_copies(NG - 1)
+        scalar_copies_and_store(NG - 1)

@@ -22,7 +22,9 @@ FLOPS = 2 * B * V * K * C
 
 LOADS = [(0, 0, 2), (0, 2, 2), (0, 4, 4), (0, 8, 8), (0, 16, 16), (1, 0, 32)]
 STAGE_BUFS = 10
-SCALAR_COPIES = [0, 0, 0, 0, 0, 0, 1, 0, 1, 0, 1, 0, 1, 1, 2, 1, 1]
+SCALAR_COPIES = [1 if g >= 10 or (g >= 4 and g % 2 == 0) else 0 for g in range(NG)]
+VECTOR_SQUARED = (0, 1)
+COEF1_PIECES = 4
 EXP1_AFTER = 3
 QUANT1_AT = 5
 
@@ -36,6 +38,7 @@ def tile_hks_t_kernel(tc, evals, evecs, count, out):
         xpool = ctx.enter_context(tc.tile_pool(name="xpool", bufs=1))
         gpool = ctx.enter_context(tc.tile_pool(name="gpool", bufs=3))
         spool = ctx.enter_context(tc.tile_pool(name="spool", bufs=STAGE_BUFS))
+        sqpool = ctx.enter_context(tc.tile_pool(name="sqpool", bufs=4))
         psum = ctx.enter_context(tc.psum_pool(name="psum", bufs=4))
         ctx.enter_context(tc.manual_schedule())
 
@@ -46,11 +49,14 @@ def tile_hks_t_kernel(tc, evals, evecs, count, out):
                 in_=evals.rearrange("b (p t) -> p b t", p=P, t=4),
             )
         words = {}
+        rows = {}
         for b, t0, n in LOADS:
             x = xpool.tile([P, n * K], BF16, name="x_%d_%d" % (b, t0))
             src = evecs[b].rearrange("(p t) k -> p (t k)", t=TILES)
             nc.sync.dma_start(out=x[:], in_=src[:, t0 * K : (t0 + n) * K])
             xw = x[:].bitcast(F32)
+            for j in range(0, n, 2):
+                rows[b * TILES + t0 + j] = x[:, j * K : (j + 2) * K]
             for j in range(n):
                 words[b * TILES + t0 + j] = xw[:, j * (K // 2) : (j + 1) * (K // 2)]
 
@@ -72,29 +78,43 @@ def tile_hks_t_kernel(tc, evals, evecs, count, out):
             )
             n *= 2
 
-        args = {}
+        exponents = consts.tile([P, 4 * B], F32, name="exponents")
+        nc.vector.tensor_scalar(out=exponents[:], in0=ev[:], scalar1=-0.01, scalar2=None, op0=ALU.mult)
+
+        exp_rows = {}
+        coef_groups = {}
         coef_codes = {}
         coef_scales = {}
 
-        def coef_args(b):
-            a = consts.tile([P, 4 * C], F32, name="arg%d" % b)
-            nc.vector.tensor_tensor(
-                out=a[:].rearrange("p (c t) -> p c t", t=4),
-                in0=powers[:].unsqueeze(2).to_broadcast([P, C, 4]),
-                in1=ev[:, 4 * b : 4 * b + 4].unsqueeze(1).to_broadcast([P, C, 4]),
-                op=ALU.mult,
-            )
-            args[b] = a
-
         def coef_exp(b):
+            er = consts.tile([P, 4 * C], BF16, name="er%d" % b, align_bytes=64)
+            for t in range(4):
+                nc.scalar.activation(
+                    out=er[:, t * C : (t + 1) * C],
+                    in_=powers[:],
+                    func=ACT.Exp,
+                    scale=exponents[:, 4 * b + t : 4 * b + t + 1],
+                )
+            exp_rows[b] = er
+
+        def coef_interleave(b):
             cf = consts.tile([P, 4 * C], BF16, name="cf%d" % b, align_bytes=64)
-            nc.scalar.activation(out=cf[:], in_=args[b][:], func=ACT.Exp, scale=-0.01)
-            args[b] = cf
+            dst = cf[:].rearrange("p (c t) -> p c t", t=4)
+            src = exp_rows[b][:].rearrange("p (t c) -> p c t", t=4)
+            if b == 0:
+                nc.vector.tensor_copy(out=dst, in_=src)
+            else:
+                for j in range(COEF1_PIECES):
+                    cols = slice(j * C // COEF1_PIECES, (j + 1) * C // COEF1_PIECES)
+                    nc.gpsimd.tensor_scalar(
+                        out=dst[:, cols, :], in0=src[:, cols, :], scalar1=1.0, scalar2=0.0, op0=ALU.mult, op1=ALU.add
+                    )
+            coef_groups[b] = cf
 
         def coef_quant(b):
             cc = consts.tile([P, C], U32, name="cc%d" % b, align_bytes=64)
             cs = consts.tile([P, C], U8, name="cs%d" % b, align_bytes=64)
-            nc.vector.quantize_mx(out=cc[:].bitcast(FP8X4), scales=cs[:], in_=args[b][:])
+            nc.vector.quantize_mx(out=cc[:].bitcast(FP8X4), scales=cs[:], in_=coef_groups[b][:])
             coef_codes[b] = cc
             coef_scales[b] = cs
 
@@ -103,6 +123,14 @@ def tile_hks_t_kernel(tc, evals, evecs, count, out):
         codes = {}
         scales = {}
         accs = {}
+
+        def presquare(pair):
+                t = 2 * pair
+                sq = sqpool.tile([P, 2 * K], BF16, name="sq", tag="sq")
+                nc.vector.tensor_tensor(out=sq[:], in0=rows[t], in1=rows[t], op=ALU.mult)
+                sqw = sq[:].bitcast(F32)
+                words[t] = sqw[:, 0 : K // 2]
+                words[t + 1] = sqw[:, K // 2 : K]
 
         def transposes(g):
             banks[g] = []
@@ -118,6 +146,12 @@ def tile_hks_t_kernel(tc, evals, evecs, count, out):
         def squares(g):
             grp = gpool.tile([P, GROUPS[g] * K], BF16, name="grouped", tag="grouped", align_bytes=64)
             for h in range(GROUPS[g] // 2):
+                if FIRST[g] // 2 + h in VECTOR_SQUARED:
+                    nc.scalar.copy(
+                        out=grp[:, h * 1024 : (h + 1) * 1024].bitcast(F32).rearrange("p (c u) -> p c u", u=2),
+                        in_=banks[g][h][:].rearrange("p (u c) -> p c u", u=2),
+                    )
+                    continue
                 nc.scalar.activation(
                     out=grp[:, h * 1024 : (h + 1) * 1024].rearrange("p (c u e) -> p c u e", u=2, e=2),
                     in_=banks[g][h][:].bitcast(BF16).rearrange("p (u c e) -> p c u e", u=2, e=2),
@@ -165,16 +199,17 @@ def tile_hks_t_kernel(tc, evals, evecs, count, out):
             dram = out[b].rearrange("(p t) c -> p (t c)", t=TILES)
             nc.sync.dma_start(out=dram[:, t0 * C : (t0 + GROUPS[g]) * C], in_=stage[:])
 
-        coef_args(0)
-        coef_args(1)
+        coef_exp(0)
+        for pair in VECTOR_SQUARED:
+            presquare(pair)
+        coef_interleave(0)
         transposes(0)
         transposes(1)
         squares(0)
-        coef_exp(0)
         for g in range(NG):
-            quantise(g)
             if g == 0:
                 coef_quant(0)
+            quantise(g)
             if g + 2 < NG:
                 transposes(g + 2)
             if g > 0:
@@ -187,6 +222,7 @@ def tile_hks_t_kernel(tc, evals, evecs, count, out):
                 scalar_copies_and_store(g - 1)
             if g == EXP1_AFTER:
                 coef_exp(1)
+                coef_interleave(1)
             multiply(g)
         vector_copies(NG - 1)
         scalar_copies_and_store(NG - 1)

@@ -22,11 +22,11 @@ FLOPS = 2 * B * V * K * C
 
 LOADS = [(0, 0, 2), (0, 2, 2), (0, 4, 4), (0, 8, 8), (0, 16, 16), (1, 0, 32)]
 STAGE_BUFS = 10
-SCALAR_COPIES = [1 if g >= 10 or (g >= 4 and g % 2 == 0) else 0 for g in range(NG)]
+SCALAR_COPIES = [1 if g >= 10 or (g >= 2 and g % 2 == 0) else 0 for g in range(NG)]
 VECTOR_SQUARED = (0, 1)
-COEF1_PIECES = 4
 EXP1_AFTER = 3
-QUANT1_AT = 5
+INTERLEAVE1_AFTER = 4
+QUANT1_AT = 6
 
 
 def tile_hks_t_kernel(tc, evals, evecs, count, out):
@@ -101,14 +101,7 @@ def tile_hks_t_kernel(tc, evals, evecs, count, out):
             cf = consts.tile([P, 4 * C], BF16, name="cf%d" % b, align_bytes=64)
             dst = cf[:].rearrange("p (c t) -> p c t", t=4)
             src = exp_rows[b][:].rearrange("p (t c) -> p c t", t=4)
-            if b == 0:
-                nc.vector.tensor_copy(out=dst, in_=src)
-            else:
-                for j in range(COEF1_PIECES):
-                    cols = slice(j * C // COEF1_PIECES, (j + 1) * C // COEF1_PIECES)
-                    nc.gpsimd.tensor_scalar(
-                        out=dst[:, cols, :], in0=src[:, cols, :], scalar1=1.0, scalar2=0.0, op0=ALU.mult, op1=ALU.add
-                    )
+            nc.vector.tensor_copy(out=dst, in_=src)
             coef_groups[b] = cf
 
         def coef_quant(b):
@@ -222,6 +215,7 @@ def tile_hks_t_kernel(tc, evals, evecs, count, out):
                 scalar_copies_and_store(g - 1)
             if g == EXP1_AFTER:
                 coef_exp(1)
+            if g == INTERLEAVE1_AFTER:
                 coef_interleave(1)
             multiply(g)
         vector_copies(NG - 1)

@@ -22,8 +22,9 @@ FLOPS = 2 * B * V * K * C
 
 LOADS = [(0, 0, 2), (0, 2, 2), (0, 4, 4), (0, 8, 8), (0, 16, 16), (1, 0, 32)]
 STAGE_BUFS = 10
-SCALAR_COPIES = [1 if g >= 10 or (g >= 2 and g % 2 == 0) else 0 for g in range(NG)]
-VECTOR_SQUARED = (0, 1)
+SCALAR_COPIES = [1 if g > 2 and g % 3 != 2 else 0 for g in range(NG)]
+VECTOR_SQUARED = (0, 1, 2)
+WARM = (12, 2, 2)
 EXP1_AFTER = 3
 INTERLEAVE1_AFTER = 4
 QUANT1_AT = 6
@@ -44,7 +45,7 @@ def tile_hks_t_kernel(tc, evals, evecs, count, out):
 
         ev = consts.tile([P, 4 * B], BF16, name="ev")
         with nc.allow_non_contiguous_dma(reason="evals: four neighbouring values to a partition"):
-            nc.sync.dma_start(
+            nc.scalar.dma_start(
                 out=ev[:].rearrange("p (b t) -> p b t", b=B, t=4),
                 in_=evals.rearrange("b (p t) -> p b t", p=P, t=4),
             )
@@ -60,6 +61,8 @@ def tile_hks_t_kernel(tc, evals, evecs, count, out):
             for j in range(n):
                 words[b * TILES + t0 + j] = xw[:, j * (K // 2) : (j + 1) * (K // 2)]
 
+        ones = consts.tile([P, C], BF16, name="ones")
+        nc.gpsimd.memset(ones[:], 1.0)
         ident = consts.tile([P, P], F32, name="ident")
         make_identity(nc, ident[:])
 
@@ -136,6 +139,11 @@ def tile_hks_t_kernel(tc, evals, evecs, count, out):
                         nc.tensor.transpose(xt[:, lo : lo + P], src[:, u : K // 2 : 2], ident[:])
                 banks[g].append(xt)
 
+        def warm_up(n):
+            dummy = psum.tile([P, C], F32, name="acc", tag="acc")
+            for i in range(n):
+                nc.tensor.matmul(out=dummy[:], lhsT=ones[:, 0:P], rhs=ones[:], start=True, stop=True)
+
         def squares(g):
             grp = gpool.tile([P, GROUPS[g] * K], BF16, name="grouped", tag="grouped", align_bytes=64)
             for h in range(GROUPS[g] // 2):
@@ -196,8 +204,11 @@ def tile_hks_t_kernel(tc, evals, evecs, count, out):
         for pair in VECTOR_SQUARED:
             presquare(pair)
         coef_interleave(0)
+        warm_up(WARM[0])
         transposes(0)
+        warm_up(WARM[1])
         transposes(1)
+        warm_up(WARM[2])
         squares(0)
         for g in range(NG):
             if g == 0:

from contextlib import ExitStack

import concourse.mybir as mybir
from concourse.masks import make_identity

F32 = mybir.dt.float32
BF16 = mybir.dt.bfloat16
U32 = mybir.dt.uint32
U8 = mybir.dt.uint8
FP8X4 = mybir.dt.float8_e4m3fn_x4
ACT = mybir.ActivationFunctionType
ALU = mybir.AluOpType

P = 128
B, V, K, C = 2, 4096, 512, 512
TILES = V // P
GROUPS = [4] * 15 + [2, 2]
NG = len(GROUPS)
FIRST = [sum(GROUPS[:g]) for g in range(NG)]

FLOPS = 2 * B * V * K * C

LOADS = [(0, 0, 2), (0, 2, 2), (0, 4, 4), (0, 8, 8), (0, 16, 16), (1, 0, 32)]
STAGE_BUFS = 10
SCALAR_COPIES = [1 if g > 2 and g % 3 != 2 else 0 for g in range(NG)]
VECTOR_SQUARED = (0, 1, 2)
WARM = (12, 2, 2)
EXP1_AFTER = 3
INTERLEAVE1_AFTER = 4
QUANT1_AT = 6


def tile_hks_t_kernel(tc, evals, evecs, count, out):
    nc = tc.nc
    assert tuple(evecs.shape) == (B, V, K) and count == C

    with ExitStack() as ctx:
        consts = ctx.enter_context(tc.tile_pool(name="consts", bufs=1))
        xpool = ctx.enter_context(tc.tile_pool(name="xpool", bufs=1))
        gpool = ctx.enter_context(tc.tile_pool(name="gpool", bufs=3))
        spool = ctx.enter_context(tc.tile_pool(name="spool", bufs=STAGE_BUFS))
        sqpool = ctx.enter_context(tc.tile_pool(name="sqpool", bufs=4))
        psum = ctx.enter_context(tc.psum_pool(name="psum", bufs=4))
        ctx.enter_context(tc.manual_schedule())

        ev = consts.tile([P, 4 * B], BF16, name="ev")
        with nc.allow_non_contiguous_dma(reason="evals: four neighbouring values to a partition"):
            nc.scalar.dma_start(
                out=ev[:].rearrange("p (b t) -> p b t", b=B, t=4),
                in_=evals.rearrange("b (p t) -> p b t", p=P, t=4),
            )
        words = {}
        rows = {}
        for b, t0, n in LOADS:
            x = xpool.tile([P, n * K], BF16, name="x_%d_%d" % (b, t0))
            src = evecs[b].rearrange("(p t) k -> p (t k)", t=TILES)
            nc.sync.dma_start(out=x[:], in_=src[:, t0 * K : (t0 + n) * K])
            xw = x[:].bitcast(F32)
            for j in range(0, n, 2):
                rows[b * TILES + t0 + j] = x[:, j * K : (j + 2) * K]
            for j in range(n):
                words[b * TILES + t0 + j] = xw[:, j * (K // 2) : (j + 1) * (K // 2)]

        ones = consts.tile([P, C], BF16, name="ones")
        nc.gpsimd.memset(ones[:], 1.0)
        ident = consts.tile([P, P], F32, name="ident")
        make_identity(nc, ident[:])

        powers = consts.tile([P, C], F32, name="powers")
        nc.vector.memset(powers[:, 0:1], 1.0)
        warm = consts.tile([P, 1], F32, name="warm")
        nc.scalar.activation(out=warm[:], in_=powers[:, 0:1], func=ACT.Exp)
        n = 1
        while n < C:
            nc.vector.tensor_scalar(
                out=powers[:, n : 2 * n],
                in0=powers[:, 0:n],
                scalar1=10.0 ** (2.0 * n / (C - 1)),
                scalar2=None,
                op0=ALU.mult,
            )
            n *= 2

        exponents = consts.tile([P, 4 * B], F32, name="exponents")
        nc.vector.tensor_scalar(out=exponents[:], in0=ev[:], scalar1=-0.01, scalar2=None, op0=ALU.mult)

        exp_rows = {}
        coef_groups = {}
        coef_codes = {}
        coef_scales = {}

        def coef_exp(b):
            er = consts.tile([P, 4 * C], BF16, name="er%d" % b, align_bytes=64)
            for t in range(4):
                nc.scalar.activation(
                    out=er[:, t * C : (t + 1) * C],
                    in_=powers[:],
                    func=ACT.Exp,
                    scale=exponents[:, 4 * b + t : 4 * b + t + 1],
                )
            exp_rows[b] = er

        def coef_interleave(b):
            cf = consts.tile([P, 4 * C], BF16, name="cf%d" % b, align_bytes=64)
            dst = cf[:].rearrange("p (c t) -> p c t", t=4)
            src = exp_rows[b][:].rearrange("p (t c) -> p c t", t=4)
            nc.vector.tensor_copy(out=dst, in_=src)
            coef_groups[b] = cf

        def coef_quant(b):
            cc = consts.tile([P, C], U32, name="cc%d" % b, align_bytes=64)
            cs = consts.tile([P, C], U8, name="cs%d" % b, align_bytes=64)
            nc.vector.quantize_mx(out=cc[:].bitcast(FP8X4), scales=cs[:], in_=coef_groups[b][:])
            coef_codes[b] = cc
            coef_scales[b] = cs

        banks = {}
        grouped = {}
        codes = {}
        scales = {}
        accs = {}

        def presquare(pair):
                t = 2 * pair
                sq = sqpool.tile([P, 2 * K], BF16, name="sq", tag="sq")
                nc.vector.tensor_tensor(out=sq[:], in0=rows[t], in1=rows[t], op=ALU.mult)
                sqw = sq[:].bitcast(F32)
                words[t] = sqw[:, 0 : K // 2]
                words[t + 1] = sqw[:, K // 2 : K]

        def transposes(g):
            banks[g] = []
            for h in range(GROUPS[g] // 2):
                xt = psum.tile([P, 512], F32, name="xt", tag="xt")
                for vt in range(2):
                    src = words[FIRST[g] + 2 * h + vt]
                    for u in range(2):
                        lo = u * 256 + vt * P
                        nc.tensor.transpose(xt[:, lo : lo + P], src[:, u : K // 2 : 2], ident[:])
                banks[g].append(xt)

        def warm_up(n):
            dummy = psum.tile([P, C], F32, name="acc", tag="acc")
            for i in range(n):
                nc.tensor.matmul(out=dummy[:], lhsT=ones[:, 0:P], rhs=ones[:], start=True, stop=True)

        def squares(g):
            grp = gpool.tile([P, GROUPS[g] * K], BF16, name="grouped", tag="grouped", align_bytes=64)
            for h in range(GROUPS[g] // 2):
                if FIRST[g] // 2 + h in VECTOR_SQUARED:
                    nc.scalar.copy(
                        out=grp[:, h * 1024 : (h + 1) * 1024].bitcast(F32).rearrange("p (c u) -> p c u", u=2),
                        in_=banks[g][h][:].rearrange("p (u c) -> p c u", u=2),
                    )
                    continue
                nc.scalar.activation(
                    out=grp[:, h * 1024 : (h + 1) * 1024].rearrange("p (c u e) -> p c u e", u=2, e=2),
                    in_=banks[g][h][:].bitcast(BF16).rearrange("p (u c e) -> p c u e", u=2, e=2),
                    func=ACT.Square,
                )
            grouped[g] = grp

        def quantise(g):
            cd = gpool.tile([P, GROUPS[g] * P], U32, name="codes", tag="codes", align_bytes=64)
            sc = gpool.tile([P, GROUPS[g] * P], U8, name="scales", tag="scales", align_bytes=64)
            nc.vector.quantize_mx(out=cd[:].bitcast(FP8X4), scales=sc[:], in_=grouped[g][:])
            codes[g] = cd
            scales[g] = sc

        def multiply(g):
            b = FIRST[g] // TILES
            accs[g] = []
            for j in range(GROUPS[g]):
                acc = psum.tile([P, C], F32, name="acc", tag="acc")
                nc.tensor.matmul_mx(
                    out=acc[:],
                    lhsT=codes[g][:, j * P : (j + 1) * P].bitcast(FP8X4),
                    lhsT_scale=scales[g][:, j * P : (j + 1) * P],
                    rhs=coef_codes[b][:].bitcast(FP8X4),
                    rhs_scale=coef_scales[b][:],
                    start=True,
                    stop=True,
                )
                accs[g].append(acc)

        stages = {}

        def vector_copies(g):
            stage = spool.tile([P, GROUPS[g] * C], F32, name="stage", tag="stage")
            for j in range(GROUPS[g] - SCALAR_COPIES[g]):
                nc.vector.tensor_copy(out=stage[:, j * C : (j + 1) * C], in_=accs[g][j][:])
            stages[g] = stage

        def scalar_copies_and_store(g):
            b = FIRST[g] // TILES
            t0 = FIRST[g] % TILES
            stage = stages[g]
            for j in range(GROUPS[g] - SCALAR_COPIES[g], GROUPS[g]):
                nc.scalar.copy(out=stage[:, j * C : (j + 1) * C], in_=accs[g][j][:])
            dram = out[b].rearrange("(p t) c -> p (t c)", t=TILES)
            nc.sync.dma_start(out=dram[:, t0 * C : (t0 + GROUPS[g]) * C], in_=stage[:])

        coef_exp(0)
        for pair in VECTOR_SQUARED:
            presquare(pair)
        coef_interleave(0)
        warm_up(WARM[0])
        transposes(0)
        warm_up(WARM[1])
        transposes(1)
        warm_up(WARM[2])
        squares(0)
        for g in range(NG):
            if g == 0:
                coef_quant(0)
            quantise(g)
            if g + 2 < NG:
                transposes(g + 2)
            if g > 0:
                vector_copies(g - 1)
            if g == QUANT1_AT:
                coef_quant(1)
            if g + 1 < NG:
                squares(g + 1)
            if g > 0:
                scalar_copies_and_store(g - 1)
            if g == EXP1_AFTER:
                coef_exp(1)
            if g == INTERLEAVE1_AFTER:
                coef_interleave(1)
            multiply(g)
        vector_copies(NG - 1)
        scalar_copies_and_store(NG - 1)
